import numpy as np
import ml_dtypes


def mxq(x, axis, fmt="e4m3"):
    dtype, down = {"e4m3": (ml_dtypes.float8_e4m3fn, 7), "e5m2": (ml_dtypes.float8_e5m2, 14)}[fmt]
    v = np.moveaxis(np.asarray(x, np.float32).astype(ml_dtypes.bfloat16).astype(np.float64), axis, -1)
    blocks = v.reshape(v.shape[:-1] + (-1, 32))
    amax = np.abs(blocks).max(-1, keepdims=True)
    byte = np.maximum(np.where(amax > 0, np.frexp(amax)[1] - 1 + 127, 0) - down, 1)
    scale = np.exp2(byte - 127.0)
    codes = (blocks / scale).astype(np.float32).astype(dtype).astype(np.float64)
    return np.moveaxis((codes * scale).reshape(v.shape), -1, axis)


WIDE = False


def mx_kscale(k):
    if not WIDE:
        return np.ones(k)
    levels = np.array([10, -10, 5, -5, 0])
    a = np.random.permutation(np.resize(levels, k // 512 * 4)).reshape(k // 512, 4)
    idx = np.arange(k)
    return np.exp2(a[idx // 512, idx % 128 // 32])


BF16 = ml_dtypes.bfloat16


def bf(x):
    return np.asarray(x, np.float32).astype(BF16)


def f64(x):
    return np.asarray(x).astype(np.float64)


R, C, E, H = 4, 512, 512, 4
D = E // H
RD = R * D


def setup_inputs():
    s = mx_kscale(E)
    t = mx_kscale(E)
    g = 1.5 / np.sqrt(E)
    return {"x": bf(np.random.standard_normal((R, C, E)) * s),
            "mask": bf(np.random.uniform(size=(R, C)) < 0.1),
            "Wq": bf(np.random.standard_normal((E, E)) * g / s[:, None] * t),
            "bq": bf(np.random.standard_normal(E) * 0.1 * t),
            "Wk": bf(np.random.standard_normal((E, E)) * g / s[:, None] / t),
            "bk": bf(np.random.standard_normal(E) * 0.1 / t)}


def reference(x, mask, Wq, bq, Wk, bk):
    scaling = (D ** -0.5) / np.sqrt(R)
    xq = mxq(f64(x), 2, "e4m3")
    q = ((xq @ mxq(f64(Wq), 0, "e4m3")) + f64(bq)).reshape(R, C, H, D)
    k = ((xq @ mxq(f64(Wk), 0, "e4m3")) + f64(bk)).reshape(R, C, H, D)
    q = q * scaling
    q = q * (1.0 - f64(mask)[:, :, None, None])
    qm = q.transpose(2, 1, 0, 3).reshape(H, C, RD)
    km = k.transpose(2, 1, 0, 3).reshape(H, C, RD)
    return mxq(qm, 2, "e4m3") @ mxq(km, 2, "e4m3").transpose(0, 2, 1)

@@ -1,0 +1,215 @@
+import math
+from contextlib import ExitStack
+
+import concourse.mybir as mybir
+from concourse.masks import make_identity
+
+F32 = mybir.dt.float32
+BF16 = mybir.dt.bfloat16
+U32 = mybir.dt.uint32
+U8 = mybir.dt.uint8
+FP8X4 = mybir.dt.float8_e4m3fn_x4
+ACT = mybir.ActivationFunctionType
+ALU = mybir.AluOpType
+
+P = 128
+PACK = 4
+R, C, E, H = 4, 512, 512, 4
+D = E // H
+CHUNKS = C // P
+TOKENS = R * P
+SCALING = (D ** -0.5) / math.sqrt(R)
+FLOPS = 2 * R * C * E * 2 * E + 2 * H * C * C * R * D
+
+BQ_ROW = 0
+BK_ROW = H
+MASK_ROW = 2 * H
+
+
+def tile_rowselfattention_pa_kernel(tc, x, mask, Wq, bq, Wk, bk, out):
+    nc = tc.nc
+    with ExitStack() as ctx:
+        keep = ctx.enter_context(tc.tile_pool(name="keep", bufs=1))
+        stores = ctx.enter_context(tc.tile_pool(name="stores", bufs=4))
+        psum_in = ctx.enter_context(tc.psum_pool(name="psum_in", bufs=2))
+        psum_proj = ctx.enter_context(tc.psum_pool(name="psum_proj", bufs=2))
+        psum_out = ctx.enter_context(tc.psum_pool(name="psum_out", bufs=2))
+
+        ident_f32 = keep.tile([P, P], F32)
+        make_identity(nc, ident_f32[:])
+        ident_bf16 = keep.tile([P, P], BF16)
+        make_identity(nc, ident_bf16[:])
+
+        small = keep.tile([P, P], BF16)
+        nc.vector.memset(small[:], 0.0)
+        nc.scalar.dma_start(out=small[BQ_ROW : BQ_ROW + H, :], in_=bq.rearrange("(h d) -> h d", d=D))
+        nc.scalar.dma_start(out=small[BK_ROW : BK_ROW + H, :], in_=bk.rearrange("(h d) -> h d", d=D))
+        nc.scalar.dma_start(
+            out=small[MASK_ROW : MASK_ROW + R * CHUNKS, :],
+            in_=mask.rearrange("r (c i) -> (r c) i", i=P),
+        )
+
+        x_sb = keep.tile([P, CHUNKS, R * E], BF16)
+        w_raw = {}
+        for name in ("k", "q"):
+            w_raw[name] = keep.tile([P, PACK * E], BF16, name="w_raw_" + name)
+
+        def load_x(c):
+            nc.sync.dma_start(
+                out=x_sb[:, c, :].rearrange("p (r e) -> p r e", r=R),
+                in_=x[:, c * P : (c + 1) * P, :].rearrange("r p e -> p r e"),
+            )
+
+        def load_w(name, w):
+            nc.sync.dma_start(
+                out=w_raw[name][:].rearrange("p (u ec) -> p u ec", u=2),
+                in_=w.rearrange("(u p e) c -> p u (e c)", u=2, e=2),
+            )
+
+        load_x(0)
+        load_w("k", Wk)
+        load_w("q", Wq)
+        for c in range(1, CHUNKS):
+            load_x(c)
+
+        small_t = psum_in.tile([P, P], F32, tag="in")
+        nc.tensor.matmul(out=small_t[:], lhsT=small[:], rhs=ident_bf16[:], start=True, stop=True)
+        bias = keep.tile([P, 2 * H], F32)
+        nc.vector.tensor_copy(out=bias[:], in_=small_t[:, 0 : 2 * H])
+
+        factor = keep.tile([P, CHUNKS, P, R], F32)
+        for c in range(CHUNKS):
+            mask_all = psum_in.tile([P, R, P], F32, tag="in")
+            for r in range(R):
+                row = MASK_ROW + r * CHUNKS + c
+                nc.tensor.matmul(
+                    out=mask_all[:, r, :],
+                    lhsT=ident_bf16[:, row : row + 1].to_broadcast([P, P]),
+                    rhs=small[:],
+                    start=True,
+                    stop=True,
+                )
+            nc.scalar.activation(
+                out=factor[:, c, :, :],
+                in_=mask_all[:].rearrange("p r i -> p i r"),
+                func=ACT.Copy,
+                bias=SCALING,
+                scale=-SCALING,
+            )
+
+        w_codes = {}
+        w_scales = {}
+        for name in ("k", "q"):
+            w_grouped = keep.tile([P, E, PACK], BF16, name="w_grouped_" + name, align_bytes=64)
+            nc.vector.tensor_copy(
+                out=w_grouped[:], in_=w_raw[name][:].rearrange("p (t c) -> p c t", t=PACK)
+            )
+            w_codes[name] = keep.tile([P, E], U32, name="w_codes_" + name, align_bytes=64)
+            w_scales[name] = keep.tile([P, E], U8, name="w_scales_" + name, align_bytes=64)
+            nc.vector.quantize_mx(
+                out=w_codes[name][:].bitcast(FP8X4),
+                scales=w_scales[name][:],
+                in_=w_grouped[:].rearrange("p c t -> p (c t)"),
+            )
+
+        x_grouped = keep.tile([P, CHUNKS, TOKENS * PACK], BF16, align_bytes=64)
+        x_codes = keep.tile([P, CHUNKS, TOKENS], U32, align_bytes=64)
+        x_scales = keep.tile([P, CHUNKS, TOKENS], U8, align_bytes=64)
+
+        def prepare_x(c):
+            x_words = x_sb[:, c, :].bitcast(F32)
+            grouped_words = x_grouped[:, c, :].bitcast(F32).rearrange("p (n u) -> p n u", u=2)
+            for pair in range(R // 2):
+                x_t = psum_in.tile([P, 2, 2 * P], F32, tag="in")
+                for half in range(2):
+                    r = 2 * pair + half
+                    for u in range(2):
+                        first = (2 * r + u) * P
+                        nc.tensor.transpose(
+                            x_t[:, u, half * P : (half + 1) * P],
+                            x_words[:, first : first + P],
+                            ident_f32[:],
+                        )
+                nc.scalar.copy(
+                    out=grouped_words[:, pair * 2 * P : (pair + 1) * 2 * P, :],
+                    in_=x_t[:].rearrange("p u n -> p n u"),
+                )
+            nc.vector.quantize_mx(
+                out=x_codes[:, c, :].bitcast(FP8X4),
+                scales=x_scales[:, c, :],
+                in_=x_grouped[:, c, :],
+            )
+
+        grouped = {}
+        codes = {}
+        scales = {}
+        for name in ("k", "q"):
+            grouped[name] = keep.tile([P, H, CHUNKS, P * R], BF16, name="grouped_" + name, align_bytes=64)
+            codes[name] = keep.tile([P, H, C], U32, name="codes_" + name, align_bytes=64)
+            scales[name] = keep.tile([P, H, C], U8, name="scales_" + name, align_bytes=64)
+
+        def project(h, c):
+            heads = slice(h * D, (h + 1) * D)
+            cols = slice(c * P, (c + 1) * P)
+            acc = {}
+            for name in ("k", "q"):
+                acc[name] = psum_proj.tile([P, R, P], F32, name="acc_" + name)
+                nc.tensor.matmul_mx(
+                    out=acc[name][:].rearrange("p r i -> p (r i)"),
+                    lhsT=w_codes[name][:, heads].bitcast(FP8X4),
+                    lhsT_scale=w_scales[name][:, heads],
+                    rhs=x_codes[:, c, :].bitcast(FP8X4),
+                    rhs_scale=x_scales[:, c, :],
+                    start=True,
+                    stop=True,
+                )
+            nc.scalar.activation(
+                out=grouped["k"][:, h, c, :].rearrange("p (i r) -> p i r", r=R),
+                in_=acc["k"][:].rearrange("p r i -> p i r"),
+                func=ACT.Identity,
+                bias=bias[:, BK_ROW + h : BK_ROW + h + 1],
+                scale=1.0,
+            )
+            nc.vector.scalar_tensor_tensor(
+                out=grouped["q"][:, h, c, :].rearrange("p (i r) -> p i r", r=R),
+                in0=acc["q"][:].rearrange("p r i -> p i r"),
+                scalar=bias[:, BQ_ROW + h : BQ_ROW + h + 1],
+                in1=factor[:, c, :, :],
+                op0=ALU.add,
+                op1=ALU.mult,
+            )
+            for name in ("k", "q"):
+                nc.vector.quantize_mx(
+                    out=codes[name][:, h, cols].bitcast(FP8X4),
+                    scales=scales[name][:, h, cols],
+                    in_=grouped[name][:, h, c, :],
+                )
+
+        def logits(h):
+            for c in range(CHUNKS):
+                cols = slice(c * P, (c + 1) * P)
+                acc_out = psum_out.tile([P, C], F32)
+                nc.tensor.matmul_mx(
+                    out=acc_out[:],
+                    lhsT=codes["q"][:, h, cols].bitcast(FP8X4),
+                    lhsT_scale=scales["q"][:, h, cols],
+                    rhs=codes["k"][:, h, :].bitcast(FP8X4),
+                    rhs_scale=scales["k"][:, h, :],
+                    start=True,
+                    stop=True,
+                )
+                result = stores.tile([P, C], F32)
+                if c == CHUNKS - 1:
+                    nc.vector.tensor_copy(out=result[:], in_=acc_out[:])
+                else:
+                    nc.scalar.copy(out=result[:], in_=acc_out[:])
+                nc.sync.dma_start(out=out[h, cols, :], in_=result[:])
+
+        for h in range(H):
+            for c in range(CHUNKS):
+                if h == 0:
+                    prepare_x(c)
+                project(h, c)
+            if h > 0:
+                logits(h - 1)
+        logits(H - 1)

@@ -18,22 +18,24 @@ R, C, E, H = 4, 512, 512, 4
 D = E // H
 CHUNKS = C // P
 TOKENS = R * P
+UNITS = H * CHUNKS
+BANKS = 8
 SCALING = (D ** -0.5) / math.sqrt(R)
 FLOPS = 2 * R * C * E * 2 * E + 2 * H * C * C * R * D
 
 BQ_ROW = 0
 BK_ROW = H
 MASK_ROW = 2 * H
+K, Q = 0, 1
 
 
 def tile_rowselfattention_pa_kernel(tc, x, mask, Wq, bq, Wk, bk, out):
     nc = tc.nc
     with ExitStack() as ctx:
+        ctx.enter_context(tc.manual_schedule())
         keep = ctx.enter_context(tc.tile_pool(name="keep", bufs=1))
-        stores = ctx.enter_context(tc.tile_pool(name="stores", bufs=4))
-        psum_in = ctx.enter_context(tc.psum_pool(name="psum_in", bufs=2))
-        psum_proj = ctx.enter_context(tc.psum_pool(name="psum_proj", bufs=2))
-        psum_out = ctx.enter_context(tc.psum_pool(name="psum_out", bufs=2))
+        stores = ctx.enter_context(tc.tile_pool(name="stores", bufs=8))
+        psum = ctx.enter_context(tc.psum_pool(name="psum", bufs=BANKS))
 
         ident_f32 = keep.tile([P, P], F32)
         make_identity(nc, ident_f32[:])
@@ -42,17 +44,15 @@ def tile_rowselfattention_pa_kernel(tc, x, mask, Wq, bq, Wk, bk, out):
 
         small = keep.tile([P, P], BF16)
         nc.vector.memset(small[:], 0.0)
-        nc.scalar.dma_start(out=small[BQ_ROW : BQ_ROW + H, :], in_=bq.rearrange("(h d) -> h d", d=D))
-        nc.scalar.dma_start(out=small[BK_ROW : BK_ROW + H, :], in_=bk.rearrange("(h d) -> h d", d=D))
-        nc.scalar.dma_start(
+        nc.sync.dma_start(out=small[BQ_ROW : BQ_ROW + H, :], in_=bq.rearrange("(h d) -> h d", d=D))
+        nc.sync.dma_start(out=small[BK_ROW : BK_ROW + H, :], in_=bk.rearrange("(h d) -> h d", d=D))
+        nc.sync.dma_start(
             out=small[MASK_ROW : MASK_ROW + R * CHUNKS, :],
             in_=mask.rearrange("r (c i) -> (r c) i", i=P),
         )
 
         x_sb = keep.tile([P, CHUNKS, R * E], BF16)
-        w_raw = {}
-        for name in ("k", "q"):
-            w_raw[name] = keep.tile([P, PACK * E], BF16, name="w_raw_" + name)
+        w_raw = keep.tile([P, 2, PACK, E], BF16)
 
         def load_x(c):
             nc.sync.dma_start(
@@ -60,26 +60,29 @@ def tile_rowselfattention_pa_kernel(tc, x, mask, Wq, bq, Wk, bk, out):
                 in_=x[:, c * P : (c + 1) * P, :].rearrange("r p e -> p r e"),
             )
 
-        def load_w(name, w):
-            nc.sync.dma_start(
-                out=w_raw[name][:].rearrange("p (u ec) -> p u ec", u=2),
-                in_=w.rearrange("(u p e) c -> p u (e c)", u=2, e=2),
-            )
+        def load_w(h):
+            head = slice(h * D, (h + 1) * D)
+            for which, w in ((K, Wk), (Q, Wq)):
+                nc.sync.dma_start(
+                    out=w_raw[:, which, :, head],
+                    in_=w[:, head].rearrange("(p t) d -> p t d", t=PACK),
+                )
 
         load_x(0)
-        load_w("k", Wk)
-        load_w("q", Wq)
+        load_w(0)
         for c in range(1, CHUNKS):
             load_x(c)
+        for h in range(1, H):
+            load_w(h)
 
-        small_t = psum_in.tile([P, P], F32, tag="in")
+        small_t = psum.tile([P, P], F32, tag="bank")
         nc.tensor.matmul(out=small_t[:], lhsT=small[:], rhs=ident_bf16[:], start=True, stop=True)
         bias = keep.tile([P, 2 * H], F32)
-        nc.vector.tensor_copy(out=bias[:], in_=small_t[:, 0 : 2 * H])
+        nc.scalar.activation(out=bias[:], in_=small_t[:, 0 : 2 * H], func=ACT.Identity)
 
         factor = keep.tile([P, CHUNKS, P, R], F32)
         for c in range(CHUNKS):
-            mask_all = psum_in.tile([P, R, P], F32, tag="in")
+            mask_all = psum.tile([P, R, P], F32, tag="bank")
             for r in range(R):
                 row = MASK_ROW + r * CHUNKS + c
                 nc.tensor.matmul(
@@ -89,27 +92,37 @@ def tile_rowselfattention_pa_kernel(tc, x, mask, Wq, bq, Wk, bk, out):
                     start=True,
                     stop=True,
                 )
-            nc.scalar.activation(
-                out=factor[:, c, :, :],
-                in_=mask_all[:].rearrange("p r i -> p i r"),
-                func=ACT.Copy,
-                bias=SCALING,
-                scale=-SCALING,
-            )
+            if c % 2 == 0:
+                nc.scalar.activation(
+                    out=factor[:, c, :, :],
+                    in_=mask_all[:].rearrange("p r i -> p i r"),
+                    func=ACT.Copy,
+                    bias=SCALING,
+                    scale=-SCALING,
+                )
+            else:
+                nc.vector.tensor_scalar(
+                    out=factor[:, c, :, :],
+                    in0=mask_all[:].rearrange("p r i -> p i r"),
+                    scalar1=-SCALING,
+                    scalar2=SCALING,
+                    op0=ALU.mult,
+                    op1=ALU.add,
+                )
 
-        w_codes = {}
-        w_scales = {}
-        for name in ("k", "q"):
-            w_grouped = keep.tile([P, E, PACK], BF16, name="w_grouped_" + name, align_bytes=64)
+        w_grouped = keep.tile([P, H, 2, D, PACK], BF16, align_bytes=64)
+        w_codes = keep.tile([P, H, 2, D], U32, align_bytes=64)
+        w_scales = keep.tile([P, H, 2, D], U8, align_bytes=64)
+
+        def prepare_w(h):
             nc.vector.tensor_copy(
-                out=w_grouped[:], in_=w_raw[name][:].rearrange("p (t c) -> p c t", t=PACK)
+                out=w_grouped[:, h, :, :, :],
+                in_=w_raw[:, :, :, h * D : (h + 1) * D].rearrange("p n t d -> p n d t"),
             )
-            w_codes[name] = keep.tile([P, E], U32, name="w_codes_" + name, align_bytes=64)
-            w_scales[name] = keep.tile([P, E], U8, name="w_scales_" + name, align_bytes=64)
             nc.vector.quantize_mx(
-                out=w_codes[name][:].bitcast(FP8X4),
-                scales=w_scales[name][:],
-                in_=w_grouped[:].rearrange("p c t -> p (c t)"),
+                out=w_codes[:, h, :, :].rearrange("p n d -> p (n d)").bitcast(FP8X4),
+                scales=w_scales[:, h, :, :].rearrange("p n d -> p (n d)"),
+                in_=w_grouped[:, h, :, :, :].rearrange("p n d t -> p (n d t)"),
             )
 
         x_grouped = keep.tile([P, CHUNKS, TOKENS * PACK], BF16, align_bytes=64)
@@ -117,18 +130,15 @@ def tile_rowselfattention_pa_kernel(tc, x, mask, Wq, bq, Wk, bk, out):
         x_scales = keep.tile([P, CHUNKS, TOKENS], U8, align_bytes=64)
 
         def prepare_x(c):
-            x_words = x_sb[:, c, :].bitcast(F32)
+            x_words = x_sb[:, c, :].bitcast(F32).rearrange("i (r p u) -> i r u p", r=R, u=2)
             grouped_words = x_grouped[:, c, :].bitcast(F32).rearrange("p (n u) -> p n u", u=2)
             for pair in range(R // 2):
-                x_t = psum_in.tile([P, 2, 2 * P], F32, tag="in")
+                x_t = psum.tile([P, 2, 2 * P], F32, tag="bank")
                 for half in range(2):
                     r = 2 * pair + half
                     for u in range(2):
-                        first = (2 * r + u) * P
                         nc.tensor.transpose(
-                            x_t[:, u, half * P : (half + 1) * P],
-                            x_words[:, first : first + P],
-                            ident_f32[:],
+                            x_t[:, u, half * P : (half + 1) * P], x_words[:, r, u, :], ident_f32[:]
                         )
                 nc.scalar.copy(
                     out=grouped_words[:, pair * 2 * P : (pair + 1) * 2 * P, :],
@@ -140,76 +150,78 @@ def tile_rowselfattention_pa_kernel(tc, x, mask, Wq, bq, Wk, bk, out):
                 in_=x_grouped[:, c, :],
             )
 
-        grouped = {}
-        codes = {}
-        scales = {}
-        for name in ("k", "q"):
-            grouped[name] = keep.tile([P, H, CHUNKS, P * R], BF16, name="grouped_" + name, align_bytes=64)
-            codes[name] = keep.tile([P, H, C], U32, name="codes_" + name, align_bytes=64)
-            scales[name] = keep.tile([P, H, C], U8, name="scales_" + name, align_bytes=64)
+        grouped = keep.tile([P, 2, H, CHUNKS, P * R], BF16, align_bytes=64)
+        codes = keep.tile([P, 2, H, C], U32, align_bytes=64)
+        scales = keep.tile([P, 2, H, C], U8, align_bytes=64)
 
         def project(h, c):
-            heads = slice(h * D, (h + 1) * D)
-            cols = slice(c * P, (c + 1) * P)
             acc = {}
-            for name in ("k", "q"):
-                acc[name] = psum_proj.tile([P, R, P], F32, name="acc_" + name)
+            for which in (K, Q):
+                acc[which] = psum.tile([P, R, P], F32, name="acc", tag="bank")
                 nc.tensor.matmul_mx(
-                    out=acc[name][:].rearrange("p r i -> p (r i)"),
-                    lhsT=w_codes[name][:, heads].bitcast(FP8X4),
-                    lhsT_scale=w_scales[name][:, heads],
+                    out=acc[which][:].rearrange("p r i -> p (r i)"),
+                    lhsT=w_codes[:, h, which, :].bitcast(FP8X4),
+                    lhsT_scale=w_scales[:, h, which, :],
                     rhs=x_codes[:, c, :].bitcast(FP8X4),
                     rhs_scale=x_scales[:, c, :],
                     start=True,
                     stop=True,
                 )
             nc.scalar.activation(
-                out=grouped["k"][:, h, c, :].rearrange("p (i r) -> p i r", r=R),
-                in_=acc["k"][:].rearrange("p r i -> p i r"),
+                out=grouped[:, K, h, c, :].rearrange("p (i r) -> p i r", r=R),
+                in_=acc[K][:].rearrange("p r i -> p i r"),
                 func=ACT.Identity,
                 bias=bias[:, BK_ROW + h : BK_ROW + h + 1],
                 scale=1.0,
             )
             nc.vector.scalar_tensor_tensor(
-                out=grouped["q"][:, h, c, :].rearrange("p (i r) -> p i r", r=R),
-                in0=acc["q"][:].rearrange("p r i -> p i r"),
+                out=grouped[:, Q, h, c, :].rearrange("p (i r) -> p i r", r=R),
+                in0=acc[Q][:].rearrange("p r i -> p i r"),
                 scalar=bias[:, BQ_ROW + h : BQ_ROW + h + 1],
                 in1=factor[:, c, :, :],
                 op0=ALU.add,
                 op1=ALU.mult,
             )
-            for name in ("k", "q"):
+
+        def quantise(h, c):
+            cols = slice(c * P, (c + 1) * P)
+            for which in (K, Q):
                 nc.vector.quantize_mx(
-                    out=codes[name][:, h, cols].bitcast(FP8X4),
-                    scales=scales[name][:, h, cols],
-                    in_=grouped[name][:, h, c, :],
+                    out=codes[:, which, h, cols].bitcast(FP8X4),
+                    scales=scales[:, which, h, cols],
+                    in_=grouped[:, which, h, c, :],
                 )
 
-        def logits(h):
-            for c in range(CHUNKS):
-                cols = slice(c * P, (c + 1) * P)
-                acc_out = psum_out.tile([P, C], F32)
-                nc.tensor.matmul_mx(
-                    out=acc_out[:],
-                    lhsT=codes["q"][:, h, cols].bitcast(FP8X4),
-                    lhsT_scale=scales["q"][:, h, cols],
-                    rhs=codes["k"][:, h, :].bitcast(FP8X4),
-                    rhs_scale=scales["k"][:, h, :],
-                    start=True,
-                    stop=True,
-                )
-                result = stores.tile([P, C], F32)
-                if c == CHUNKS - 1:
-                    nc.vector.tensor_copy(out=result[:], in_=acc_out[:])
-                else:
-                    nc.scalar.copy(out=result[:], in_=acc_out[:])
-                nc.sync.dma_start(out=out[h, cols, :], in_=result[:])
+        def logits(h, c):
+            cols = slice(c * P, (c + 1) * P)
+            acc_out = psum.tile([P, C], F32, tag="bank")
+            nc.tensor.matmul_mx(
+                out=acc_out[:],
+                lhsT=codes[:, Q, h, cols].bitcast(FP8X4),
+                lhsT_scale=scales[:, Q, h, cols],
+                rhs=codes[:, K, h, :].bitcast(FP8X4),
+                rhs_scale=scales[:, K, h, :],
+                start=True,
+                stop=True,
+            )
+            result = stores.tile([P, C], F32)
+            if h == H - 1 and c % 2 == 1:
+                nc.vector.tensor_copy(out=result[:], in_=acc_out[:])
+            else:
+                nc.scalar.copy(out=result[:], in_=acc_out[:])
+            nc.sync.dma_start(out=out[h, cols, :], in_=result[:])
 
-        for h in range(H):
-            for c in range(CHUNKS):
-                if h == 0:
-                    prepare_x(c)
+        prepare_w(0)
+        prepare_x(0)
+        for step in range(UNITS + CHUNKS):
+            if 1 <= step <= UNITS:
+                quantise(*divmod(step - 1, CHUNKS))
+            if step + 1 < CHUNKS:
+                prepare_x(step + 1)
+            if step < UNITS:
+                h, c = divmod(step, CHUNKS)
                 project(h, c)
-            if h > 0:
-                logits(h - 1)
-        logits(H - 1)
+                if c == 0 and h + 1 < H:
+                    prepare_w(h + 1)
+            if step >= CHUNKS:
+                logits(*divmod(step - CHUNKS, CHUNKS))

@@ -20,6 +20,8 @@ CHUNKS = C // P
 TOKENS = R * P
 UNITS = H * CHUNKS
 BANKS = 8
+RUN = 4
+LOGITS_LAG = 6
 SCALING = (D ** -0.5) / math.sqrt(R)
 FLOPS = 2 * R * C * E * 2 * E + 2 * H * C * C * R * D
 
@@ -37,13 +39,13 @@ def tile_rowselfattention_pa_kernel(tc, x, mask, Wq, bq, Wk, bk, out):
         stores = ctx.enter_context(tc.tile_pool(name="stores", bufs=8))
         psum = ctx.enter_context(tc.psum_pool(name="psum", bufs=BANKS))
 
-        ident_f32 = keep.tile([P, P], F32)
-        make_identity(nc, ident_f32[:])
+        small = keep.tile([P, P], BF16)
+        nc.gpsimd.memset(small[:], 0.0)
         ident_bf16 = keep.tile([P, P], BF16)
         make_identity(nc, ident_bf16[:])
+        ident_f32 = keep.tile([P, P], F32)
+        make_identity(nc, ident_f32[:])
 
-        small = keep.tile([P, P], BF16)
-        nc.vector.memset(small[:], 0.0)
         nc.sync.dma_start(out=small[BQ_ROW : BQ_ROW + H, :], in_=bq.rearrange("(h d) -> h d", d=D))
         nc.sync.dma_start(out=small[BK_ROW : BK_ROW + H, :], in_=bk.rearrange("(h d) -> h d", d=D))
         nc.sync.dma_start(
@@ -114,11 +116,13 @@ def tile_rowselfattention_pa_kernel(tc, x, mask, Wq, bq, Wk, bk, out):
         w_codes = keep.tile([P, H, 2, D], U32, align_bytes=64)
         w_scales = keep.tile([P, H, 2, D], U8, align_bytes=64)
 
-        def prepare_w(h):
+        def regroup_w(h):
             nc.vector.tensor_copy(
-                out=w_grouped[:, h, :, :, :],
-                in_=w_raw[:, :, :, h * D : (h + 1) * D].rearrange("p n t d -> p n d t"),
+                out=w_grouped[:, h, :, :, :].rearrange("p n (g i) t -> p n g t i", i=RUN),
+                in_=w_raw[:, :, :, h * D : (h + 1) * D].rearrange("p n t (g i) -> p n g t i", i=RUN),
             )
+
+        def quantise_w(h):
             nc.vector.quantize_mx(
                 out=w_codes[:, h, :, :].rearrange("p n d -> p (n d)").bitcast(FP8X4),
                 scales=w_scales[:, h, :, :].rearrange("p n d -> p (n d)"),
@@ -192,7 +196,7 @@ def tile_rowselfattention_pa_kernel(tc, x, mask, Wq, bq, Wk, bk, out):
                     in_=grouped[:, which, h, c, :],
                 )
 
-        def logits(h, c):
+        def logits(h, c, on_vector):
             cols = slice(c * P, (c + 1) * P)
             acc_out = psum.tile([P, C], F32, tag="bank")
             nc.tensor.matmul_mx(
@@ -205,23 +209,26 @@ def tile_rowselfattention_pa_kernel(tc, x, mask, Wq, bq, Wk, bk, out):
                 stop=True,
             )
             result = stores.tile([P, C], F32)
-            if h == H - 1 and c % 2 == 1:
+            if on_vector:
                 nc.vector.tensor_copy(out=result[:], in_=acc_out[:])
             else:
                 nc.scalar.copy(out=result[:], in_=acc_out[:])
             nc.sync.dma_start(out=out[h, cols, :], in_=result[:])
 
-        prepare_w(0)
+        regroup_w(0)
+        quantise_w(0)
         prepare_x(0)
-        for step in range(UNITS + CHUNKS):
-            if 1 <= step <= UNITS:
-                quantise(*divmod(step - 1, CHUNKS))
+        for step in range(UNITS + LOGITS_LAG):
+            h, c = divmod(step, CHUNKS)
             if step + 1 < CHUNKS:
                 prepare_x(step + 1)
             if step < UNITS:
-                h, c = divmod(step, CHUNKS)
                 project(h, c)
-                if c == 0 and h + 1 < H:
-                    prepare_w(h + 1)
-            if step >= CHUNKS:
-                logits(*divmod(step - CHUNKS, CHUNKS))
+            if 1 <= step <= UNITS:
+                quantise(*divmod(step - 1, CHUNKS))
+            if h + 1 < H and c == 0:
+                regroup_w(h + 1)
+            if h + 1 < H and c == 1:
+                quantise_w(h + 1)
+            if step >= LOGITS_LAG:
+                logits(*divmod(step - LOGITS_LAG, CHUNKS), step >= UNITS and step % 2 == 0)

@@ -57,10 +57,12 @@ def tile_rowselfattention_pa_kernel(tc, x, mask, Wq, bq, Wk, bk, out):
         w_raw = keep.tile([P, 2, PACK, E], BF16)
 
         def load_x(c):
-            nc.sync.dma_start(
-                out=x_sb[:, c, :].rearrange("p (r e) -> p r e", r=R),
-                in_=x[:, c * P : (c + 1) * P, :].rearrange("r p e -> p r e"),
-            )
+            for pair in range(R // 2):
+                rows = slice(2 * pair, 2 * pair + 2)
+                nc.sync.dma_start(
+                    out=x_sb[:, c, :].rearrange("p (r e) -> p r e", r=R)[:, rows, :],
+                    in_=x[rows, c * P : (c + 1) * P, :].rearrange("r p e -> p r e"),
+                )
 
         def load_w(h):
             head = slice(h * D, (h + 1) * D)
@@ -83,7 +85,8 @@ def tile_rowselfattention_pa_kernel(tc, x, mask, Wq, bq, Wk, bk, out):
         nc.scalar.activation(out=bias[:], in_=small_t[:, 0 : 2 * H], func=ACT.Identity)
 
         factor = keep.tile([P, CHUNKS, P, R], F32)
-        for c in range(CHUNKS):
+
+        def mask_factor(c):
             mask_all = psum.tile([P, R, P], F32, tag="bank")
             for r in range(R):
                 row = MASK_ROW + r * CHUNKS + c
@@ -94,23 +97,13 @@ def tile_rowselfattention_pa_kernel(tc, x, mask, Wq, bq, Wk, bk, out):
                     start=True,
                     stop=True,
                 )
-            if c % 2 == 0:
-                nc.scalar.activation(
-                    out=factor[:, c, :, :],
-                    in_=mask_all[:].rearrange("p r i -> p i r"),
-                    func=ACT.Copy,
-                    bias=SCALING,
-                    scale=-SCALING,
-                )
-            else:
-                nc.vector.tensor_scalar(
-                    out=factor[:, c, :, :],
-                    in0=mask_all[:].rearrange("p r i -> p i r"),
-                    scalar1=-SCALING,
-                    scalar2=SCALING,
-                    op0=ALU.mult,
-                    op1=ALU.add,
-                )
+            nc.scalar.activation(
+                out=factor[:, c, :, :],
+                in_=mask_all[:].rearrange("p r i -> p i r"),
+                func=ACT.Copy,
+                bias=SCALING,
+                scale=-SCALING,
+            )
 
         w_grouped = keep.tile([P, H, 2, D, PACK], BF16, align_bytes=64)
         w_codes = keep.tile([P, H, 2, D], U32, align_bytes=64)
@@ -144,15 +137,15 @@ def tile_rowselfattention_pa_kernel(tc, x, mask, Wq, bq, Wk, bk, out):
                         nc.tensor.transpose(
                             x_t[:, u, half * P : (half + 1) * P], x_words[:, r, u, :], ident_f32[:]
                         )
+                tokens = slice(pair * 2 * P, (pair + 1) * 2 * P)
                 nc.scalar.copy(
-                    out=grouped_words[:, pair * 2 * P : (pair + 1) * 2 * P, :],
-                    in_=x_t[:].rearrange("p u n -> p n u"),
+                    out=grouped_words[:, tokens, :], in_=x_t[:].rearrange("p u n -> p n u")
                 )
-            nc.vector.quantize_mx(
-                out=x_codes[:, c, :].bitcast(FP8X4),
-                scales=x_scales[:, c, :],
-                in_=x_grouped[:, c, :],
-            )
+                nc.vector.quantize_mx(
+                    out=x_codes[:, c, tokens].bitcast(FP8X4),
+                    scales=x_scales[:, c, tokens],
+                    in_=x_grouped[:, c, pair * 2 * P * PACK : (pair + 1) * 2 * P * PACK],
+                )
 
         grouped = keep.tile([P, 2, H, CHUNKS, P * R], BF16, align_bytes=64)
         codes = keep.tile([P, 2, H, C], U32, align_bytes=64)
@@ -215,9 +208,13 @@ def tile_rowselfattention_pa_kernel(tc, x, mask, Wq, bq, Wk, bk, out):
                 nc.scalar.copy(out=result[:], in_=acc_out[:])
             nc.sync.dma_start(out=out[h, cols, :], in_=result[:])
 
+        mask_factor(0)
+        mask_factor(1)
         regroup_w(0)
         quantise_w(0)
         prepare_x(0)
+        mask_factor(2)
+        mask_factor(3)
         for step in range(UNITS + LOGITS_LAG):
             h, c = divmod(step, CHUNKS)
             if step + 1 < CHUNKS:

@@ -64,20 +64,20 @@ def tile_rowselfattention_pa_kernel(tc, x, mask, Wq, bq, Wk, bk, out):
                     in_=x[rows, c * P : (c + 1) * P, :].rearrange("r p e -> p r e"),
                 )
 
-        def load_w(h):
-            head = slice(h * D, (h + 1) * D)
+        def load_w(first, last):
+            cols = slice(first * D, last * D)
             for which, w in ((K, Wk), (Q, Wq)):
-                nc.sync.dma_start(
-                    out=w_raw[:, which, :, head],
-                    in_=w[:, head].rearrange("(p t) d -> p t d", t=PACK),
-                )
+                for u in range(2):
+                    nc.sync.dma_start(
+                        out=w_raw[:, which, 2 * u : 2 * u + 2, cols],
+                        in_=w[2 * u * P : 2 * (u + 1) * P, cols].rearrange("(p e) d -> p e d", e=2),
+                    )
 
         load_x(0)
-        load_w(0)
+        load_w(0, 1)
         for c in range(1, CHUNKS):
             load_x(c)
-        for h in range(1, H):
-            load_w(h)
+        load_w(1, H)
 
         small_t = psum.tile([P, P], F32, tag="bank")
         nc.tensor.matmul(out=small_t[:], lhsT=small[:], rhs=ident_bf16[:], start=True, stop=True)
@@ -127,7 +127,7 @@ def tile_rowselfattention_pa_kernel(tc, x, mask, Wq, bq, Wk, bk, out):
         x_scales = keep.tile([P, CHUNKS, TOKENS], U8, align_bytes=64)
 
         def prepare_x(c):
-            x_words = x_sb[:, c, :].bitcast(F32).rearrange("i (r p u) -> i r u p", r=R, u=2)
+            x_words = x_sb[:, c, :].bitcast(F32).rearrange("i (r u p) -> i r u p", r=R, u=2)
             grouped_words = x_grouped[:, c, :].bitcast(F32).rearrange("p (n u) -> p n u", u=2)
             for pair in range(R // 2):
                 x_t = psum.tile([P, 2, 2 * P], F32, tag="bank")

@@ -223,9 +223,9 @@ def tile_rowselfattention_pa_kernel(tc, x, mask, Wq, bq, Wk, bk, out):
                 project(h, c)
             if 1 <= step <= UNITS:
                 quantise(*divmod(step - 1, CHUNKS))
-            if h + 1 < H and c == 0:
+            if h + 1 < H and c == 2:
                 regroup_w(h + 1)
-            if h + 1 < H and c == 1:
+            if h + 1 < H and c == 3:
                 quantise_w(h + 1)
             if step >= LOGITS_LAG:
                 logits(*divmod(step - LOGITS_LAG, CHUNKS), step >= UNITS and step % 2 == 0)

@@ -21,7 +21,9 @@ TOKENS = R * P
 UNITS = H * CHUNKS
 BANKS = 8
 RUN = 4
-LOGITS_LAG = 6
+AHEAD = 2
+LOGITS_FIRST = CHUNKS + 2
+LOGITS_STEPS = 12
 SCALING = (D ** -0.5) / math.sqrt(R)
 FLOPS = 2 * R * C * E * 2 * E + 2 * H * C * C * R * D
 
@@ -64,20 +66,24 @@ def tile_rowselfattention_pa_kernel(tc, x, mask, Wq, bq, Wk, bk, out):
                     in_=x[rows, c * P : (c + 1) * P, :].rearrange("r p e -> p r e"),
                 )
 
-        def load_w(first, last):
+        def load_w(which, first, last):
             cols = slice(first * D, last * D)
-            for which, w in ((K, Wk), (Q, Wq)):
-                for u in range(2):
-                    nc.sync.dma_start(
-                        out=w_raw[:, which, 2 * u : 2 * u + 2, cols],
-                        in_=w[2 * u * P : 2 * (u + 1) * P, cols].rearrange("(p e) d -> p e d", e=2),
-                    )
+            w = Wk if which == K else Wq
+            for u in range(2):
+                nc.sync.dma_start(
+                    out=w_raw[:, which, 2 * u : 2 * u + 2, cols],
+                    in_=w[2 * u * P : 2 * (u + 1) * P, cols].rearrange("(p e) d -> p e d", e=2),
+                )
 
+        load_w(K, 0, 1)
         load_x(0)
-        load_w(0, 1)
+        load_w(Q, 0, 1)
         for c in range(1, CHUNKS):
             load_x(c)
-        load_w(1, H)
+        load_w(K, 1, 2)
+        load_w(Q, 1, 2)
+        load_w(K, 2, H)
+        load_w(Q, 2, H)
 
         small_t = psum.tile([P, P], F32, tag="bank")
         nc.tensor.matmul(out=small_t[:], lhsT=small[:], rhs=ident_bf16[:], start=True, stop=True)
@@ -110,10 +116,11 @@ def tile_rowselfattention_pa_kernel(tc, x, mask, Wq, bq, Wk, bk, out):
         w_scales = keep.tile([P, H, 2, D], U8, align_bytes=64)
 
         def regroup_w(h):
-            nc.vector.tensor_copy(
-                out=w_grouped[:, h, :, :, :].rearrange("p n (g i) t -> p n g t i", i=RUN),
-                in_=w_raw[:, :, :, h * D : (h + 1) * D].rearrange("p n t (g i) -> p n g t i", i=RUN),
-            )
+            for which in (K, Q):
+                nc.vector.tensor_copy(
+                    out=w_grouped[:, h, which, :, :].rearrange("p (g i) t -> p g t i", i=RUN),
+                    in_=w_raw[:, which, :, h * D : (h + 1) * D].rearrange("p t (g i) -> p g t i", i=RUN),
+                )
 
         def quantise_w(h):
             nc.vector.quantize_mx(
@@ -126,7 +133,7 @@ def tile_rowselfattention_pa_kernel(tc, x, mask, Wq, bq, Wk, bk, out):
         x_codes = keep.tile([P, CHUNKS, TOKENS], U32, align_bytes=64)
         x_scales = keep.tile([P, CHUNKS, TOKENS], U8, align_bytes=64)
 
-        def prepare_x(c):
+        def transpose_x(c):
             x_words = x_sb[:, c, :].bitcast(F32).rearrange("i (r u p) -> i r u p", r=R, u=2)
             grouped_words = x_grouped[:, c, :].bitcast(F32).rearrange("p (n u) -> p n u", u=2)
             for pair in range(R // 2):
@@ -141,55 +148,67 @@ def tile_rowselfattention_pa_kernel(tc, x, mask, Wq, bq, Wk, bk, out):
                 nc.scalar.copy(
                     out=grouped_words[:, tokens, :], in_=x_t[:].rearrange("p u n -> p n u")
                 )
-                nc.vector.quantize_mx(
-                    out=x_codes[:, c, tokens].bitcast(FP8X4),
-                    scales=x_scales[:, c, tokens],
-                    in_=x_grouped[:, c, pair * 2 * P * PACK : (pair + 1) * 2 * P * PACK],
-                )
+
+        def quantise_x(c, pair):
+            tokens = slice(pair * 2 * P, (pair + 1) * 2 * P)
+            nc.vector.quantize_mx(
+                out=x_codes[:, c, tokens].bitcast(FP8X4),
+                scales=x_scales[:, c, tokens],
+                in_=x_grouped[:, c, pair * 2 * P * PACK : (pair + 1) * 2 * P * PACK],
+            )
 
         grouped = keep.tile([P, 2, H, CHUNKS, P * R], BF16, align_bytes=64)
         codes = keep.tile([P, 2, H, C], U32, align_bytes=64)
         scales = keep.tile([P, 2, H, C], U8, align_bytes=64)
 
-        def project(h, c):
-            acc = {}
-            for which in (K, Q):
-                acc[which] = psum.tile([P, R, P], F32, name="acc", tag="bank")
-                nc.tensor.matmul_mx(
-                    out=acc[which][:].rearrange("p r i -> p (r i)"),
-                    lhsT=w_codes[:, h, which, :].bitcast(FP8X4),
-                    lhsT_scale=w_scales[:, h, which, :],
-                    rhs=x_codes[:, c, :].bitcast(FP8X4),
-                    rhs_scale=x_scales[:, c, :],
-                    start=True,
-                    stop=True,
-                )
+        accs = {}
+
+        def project(which, unit):
+            h, c = divmod(unit, CHUNKS)
+            acc = psum.tile([P, R, P], F32, tag="bank")
+            nc.tensor.matmul_mx(
+                out=acc[:].rearrange("p r i -> p (r i)"),
+                lhsT=w_codes[:, h, which, :].bitcast(FP8X4),
+                lhsT_scale=w_scales[:, h, which, :],
+                rhs=x_codes[:, c, :].bitcast(FP8X4),
+                rhs_scale=x_scales[:, c, :],
+                start=True,
+                stop=True,
+            )
+            accs[which, unit] = acc
+
+        def empty_k(unit):
+            h, c = divmod(unit, CHUNKS)
             nc.scalar.activation(
                 out=grouped[:, K, h, c, :].rearrange("p (i r) -> p i r", r=R),
-                in_=acc[K][:].rearrange("p r i -> p i r"),
+                in_=accs[K, unit][:].rearrange("p r i -> p i r"),
                 func=ACT.Identity,
                 bias=bias[:, BK_ROW + h : BK_ROW + h + 1],
                 scale=1.0,
             )
+
+        def empty_q(unit):
+            h, c = divmod(unit, CHUNKS)
             nc.vector.scalar_tensor_tensor(
                 out=grouped[:, Q, h, c, :].rearrange("p (i r) -> p i r", r=R),
-                in0=acc[Q][:].rearrange("p r i -> p i r"),
+                in0=accs[Q, unit][:].rearrange("p r i -> p i r"),
                 scalar=bias[:, BQ_ROW + h : BQ_ROW + h + 1],
                 in1=factor[:, c, :, :],
                 op0=ALU.add,
                 op1=ALU.mult,
             )
 
-        def quantise(h, c):
-            cols = slice(c * P, (c + 1) * P)
-            for which in (K, Q):
-                nc.vector.quantize_mx(
-                    out=codes[:, which, h, cols].bitcast(FP8X4),
-                    scales=scales[:, which, h, cols],
-                    in_=grouped[:, which, h, c, :],
-                )
+        def quantise(which, first, count):
+            h, c = divmod(first, CHUNKS)
+            cols = slice(c * P, (c + count) * P)
+            nc.vector.quantize_mx(
+                out=codes[:, which, h, cols].bitcast(FP8X4),
+                scales=scales[:, which, h, cols],
+                in_=grouped[:, which, h, c : c + count, :].rearrange("p c n -> p (c n)"),
+            )
 
-        def logits(h, c, on_vector):
+        def multiply(unit):
+            h, c = divmod(unit, CHUNKS)
             cols = slice(c * P, (c + 1) * P)
             acc_out = psum.tile([P, C], F32, tag="bank")
             nc.tensor.matmul_mx(
@@ -201,31 +220,55 @@ def tile_rowselfattention_pa_kernel(tc, x, mask, Wq, bq, Wk, bk, out):
                 start=True,
                 stop=True,
             )
+            accs["logits", unit] = acc_out
+
+        def store(unit):
+            h, c = divmod(unit, CHUNKS)
             result = stores.tile([P, C], F32)
-            if on_vector:
-                nc.vector.tensor_copy(out=result[:], in_=acc_out[:])
-            else:
-                nc.scalar.copy(out=result[:], in_=acc_out[:])
-            nc.sync.dma_start(out=out[h, cols, :], in_=result[:])
+            nc.scalar.copy(out=result[:], in_=accs["logits", unit][:])
+            nc.sync.dma_start(out=out[h, c * P : (c + 1) * P, :], in_=result[:])
 
         mask_factor(0)
         mask_factor(1)
+        transpose_x(0)
         regroup_w(0)
+        quantise_x(0, 0)
         quantise_w(0)
-        prepare_x(0)
         mask_factor(2)
         mask_factor(3)
-        for step in range(UNITS + LOGITS_LAG):
-            h, c = divmod(step, CHUNKS)
+        quantise_x(0, 1)
+
+        regroup_at = {1: 1, 2: 2, 6: 3}
+        k_next = 0
+        k_left = []
+        for step in range(LOGITS_FIRST + LOGITS_STEPS):
             if step + 1 < CHUNKS:
-                prepare_x(step + 1)
+                transpose_x(step + 1)
+                quantise_x(step + 1, 0)
+                quantise_x(step + 1, 1)
+            k_last = step if step < CHUNKS else min(2 * step - CHUNKS + 1, step + AHEAD)
+            k_units = list(range(k_next, min(k_last + 1, UNITS)))
+            k_next += len(k_units)
+            for unit in k_units:
+                project(K, unit)
             if step < UNITS:
-                project(h, c)
+                project(Q, step)
+            l_units = [i for i in range(UNITS) if LOGITS_FIRST + i * LOGITS_STEPS // UNITS == step]
+            for unit in l_units:
+                multiply(unit)
+            for unit in k_left:
+                if unit % 2 == 1:
+                    quantise(K, unit - 1, 2)
+            k_left = k_units
+            for unit in k_units:
+                empty_k(unit)
+            if step - 1 in regroup_at:
+                quantise_w(regroup_at[step - 1])
+            if step < UNITS:
+                empty_q(step)
             if 1 <= step <= UNITS:
-                quantise(*divmod(step - 1, CHUNKS))
-            if h + 1 < H and c == 2:
-                regroup_w(h + 1)
-            if h + 1 < H and c == 3:
-                quantise_w(h + 1)
-            if step >= LOGITS_LAG:
-                logits(*divmod(step - LOGITS_LAG, CHUNKS), step >= UNITS and step % 2 == 0)
+                quantise(Q, step - 1, 1)
+            if step in regroup_at:
+                regroup_w(regroup_at[step])
+            for unit in l_units:
+                store(unit)

@@ -23,7 +23,7 @@ BANKS = 8
 RUN = 4
 AHEAD = 2
 LOGITS_FIRST = CHUNKS + 2
-LOGITS_STEPS = 12
+LOGITS_STEPS = 13
 SCALING = (D ** -0.5) / math.sqrt(R)
 FLOPS = 2 * R * C * E * 2 * E + 2 * H * C * C * R * D
 
@@ -43,6 +43,8 @@ def tile_rowselfattention_pa_kernel(tc, x, mask, Wq, bq, Wk, bk, out):
 
         small = keep.tile([P, P], BF16)
         nc.gpsimd.memset(small[:], 0.0)
+        zeros = keep.tile([P, C], BF16)
+        nc.vector.memset(zeros[:], 0.0)
         ident_bf16 = keep.tile([P, P], BF16)
         make_identity(nc, ident_bf16[:])
         ident_f32 = keep.tile([P, P], F32)
@@ -75,8 +77,8 @@ def tile_rowselfattention_pa_kernel(tc, x, mask, Wq, bq, Wk, bk, out):
                     in_=w[2 * u * P : 2 * (u + 1) * P, cols].rearrange("(p e) d -> p e d", e=2),
                 )
 
-        load_w(K, 0, 1)
         load_x(0)
+        load_w(K, 0, 1)
         load_w(Q, 0, 1)
         for c in range(1, CHUNKS):
             load_x(c)
@@ -84,6 +86,13 @@ def tile_rowselfattention_pa_kernel(tc, x, mask, Wq, bq, Wk, bk, out):
         load_w(Q, 1, 2)
         load_w(K, 2, H)
         load_w(Q, 2, H)
+
+        def keep_warm(count):
+            unread = psum.tile([P, C], F32, tag="bank")
+            for n in range(count):
+                nc.tensor.matmul(out=unread[:], lhsT=zeros[:, 0:P], rhs=zeros[:], start=True, stop=True)
+
+        keep_warm(3)
 
         small_t = psum.tile([P, P], F32, tag="bank")
         nc.tensor.matmul(out=small_t[:], lhsT=small[:], rhs=ident_bf16[:], start=True, stop=True)
@@ -145,9 +154,8 @@ def tile_rowselfattention_pa_kernel(tc, x, mask, Wq, bq, Wk, bk, out):
                             x_t[:, u, half * P : (half + 1) * P], x_words[:, r, u, :], ident_f32[:]
                         )
                 tokens = slice(pair * 2 * P, (pair + 1) * 2 * P)
-                nc.scalar.copy(
-                    out=grouped_words[:, tokens, :], in_=x_t[:].rearrange("p u n -> p n u")
-                )
+                empty = nc.vector.tensor_copy if (c, pair) == (1, 1) else nc.scalar.copy
+                empty(out=grouped_words[:, tokens, :], in_=x_t[:].rearrange("p u n -> p n u"))
 
         def quantise_x(c, pair):
             tokens = slice(pair * 2 * P, (pair + 1) * 2 * P)
@@ -225,12 +233,16 @@ def tile_rowselfattention_pa_kernel(tc, x, mask, Wq, bq, Wk, bk, out):
         def store(unit):
             h, c = divmod(unit, CHUNKS)
             result = stores.tile([P, C], F32)
-            nc.scalar.copy(out=result[:], in_=accs["logits", unit][:])
+            if unit == UNITS - 1:
+                nc.vector.tensor_copy(out=result[:], in_=accs["logits", unit][:])
+            else:
+                nc.scalar.copy(out=result[:], in_=accs["logits", unit][:])
             nc.sync.dma_start(out=out[h, c * P : (c + 1) * P, :], in_=result[:])
 
         mask_factor(0)
         mask_factor(1)
         transpose_x(0)
+        keep_warm(2)
         regroup_w(0)
         quantise_x(0, 0)
         quantise_w(0)

@@ -21,9 +21,9 @@ TOKENS = R * P
 UNITS = H * CHUNKS
 BANKS = 8
 RUN = 4
-AHEAD = 2
-LOGITS_FIRST = CHUNKS + 2
-LOGITS_STEPS = 13
+Q_STEP = CHUNKS
+K_EARLY = 2
+LOGITS_LAG = 4
 SCALING = (D ** -0.5) / math.sqrt(R)
 FLOPS = 2 * R * C * E * 2 * E + 2 * H * C * C * R * D
 
@@ -41,32 +41,32 @@ def tile_rowselfattention_pa_kernel(tc, x, mask, Wq, bq, Wk, bk, out):
         stores = ctx.enter_context(tc.tile_pool(name="stores", bufs=8))
         psum = ctx.enter_context(tc.psum_pool(name="psum", bufs=BANKS))
 
-        small = keep.tile([P, P], BF16)
-        nc.gpsimd.memset(small[:], 0.0)
         zeros = keep.tile([P, C], BF16)
         nc.vector.memset(zeros[:], 0.0)
-        ident_bf16 = keep.tile([P, P], BF16)
-        make_identity(nc, ident_bf16[:])
+        small = keep.tile([P, P], BF16)
+        nc.gpsimd.memset(small[:], 0.0)
         ident_f32 = keep.tile([P, P], F32)
         make_identity(nc, ident_f32[:])
-
-        nc.sync.dma_start(out=small[BQ_ROW : BQ_ROW + H, :], in_=bq.rearrange("(h d) -> h d", d=D))
-        nc.sync.dma_start(out=small[BK_ROW : BK_ROW + H, :], in_=bk.rearrange("(h d) -> h d", d=D))
-        nc.sync.dma_start(
-            out=small[MASK_ROW : MASK_ROW + R * CHUNKS, :],
-            in_=mask.rearrange("r (c i) -> (r c) i", i=P),
-        )
+        ident_bf16 = keep.tile([P, P], BF16)
+        make_identity(nc, ident_bf16[:])
 
         x_sb = keep.tile([P, CHUNKS, R * E], BF16)
         w_raw = keep.tile([P, 2, PACK, E], BF16)
 
-        def load_x(c):
-            for pair in range(R // 2):
-                rows = slice(2 * pair, 2 * pair + 2)
-                nc.sync.dma_start(
-                    out=x_sb[:, c, :].rearrange("p (r e) -> p r e", r=R)[:, rows, :],
-                    in_=x[rows, c * P : (c + 1) * P, :].rearrange("r p e -> p r e"),
-                )
+        def load_x(c, pair):
+            rows = slice(2 * pair, 2 * pair + 2)
+            nc.sync.dma_start(
+                out=x_sb[:, c, :].rearrange("p (r e) -> p r e", r=R)[:, rows, :],
+                in_=x[rows, c * P : (c + 1) * P, :].rearrange("r p e -> p r e"),
+            )
+
+        def load_small():
+            nc.sync.dma_start(out=small[BQ_ROW : BQ_ROW + H, :], in_=bq.rearrange("(h d) -> h d", d=D))
+            nc.sync.dma_start(out=small[BK_ROW : BK_ROW + H, :], in_=bk.rearrange("(h d) -> h d", d=D))
+            nc.sync.dma_start(
+                out=small[MASK_ROW : MASK_ROW + R * CHUNKS, :],
+                in_=mask.rearrange("r (c i) -> (r c) i", i=P),
+            )
 
         def load_w(which, first, last):
             cols = slice(first * D, last * D)
@@ -77,31 +77,33 @@ def tile_rowselfattention_pa_kernel(tc, x, mask, Wq, bq, Wk, bk, out):
                     in_=w[2 * u * P : 2 * (u + 1) * P, cols].rearrange("(p e) d -> p e d", e=2),
                 )
 
-        load_x(0)
-        load_w(K, 0, 1)
+        load_x(0, 0)
+        load_small()
+        load_x(0, 1)
+        load_w(K, 0, H)
+        for c in (1, 2):
+            load_x(c, 0)
+            load_x(c, 1)
         load_w(Q, 0, 1)
-        for c in range(1, CHUNKS):
-            load_x(c)
-        load_w(K, 1, 2)
-        load_w(Q, 1, 2)
-        load_w(K, 2, H)
-        load_w(Q, 2, H)
+        load_x(3, 0)
+        load_x(3, 1)
+        load_w(Q, 1, H)
 
         def keep_warm(count):
             unread = psum.tile([P, C], F32, tag="bank")
             for n in range(count):
                 nc.tensor.matmul(out=unread[:], lhsT=zeros[:, 0:P], rhs=zeros[:], start=True, stop=True)
 
-        keep_warm(3)
-
-        small_t = psum.tile([P, P], F32, tag="bank")
-        nc.tensor.matmul(out=small_t[:], lhsT=small[:], rhs=ident_bf16[:], start=True, stop=True)
         bias = keep.tile([P, 2 * H], F32)
-        nc.scalar.activation(out=bias[:], in_=small_t[:, 0 : 2 * H], func=ACT.Identity)
+
+        def biases():
+            small_t = psum.tile([P, P], F32, tag="bank")
+            nc.tensor.matmul(out=small_t[:], lhsT=small[:], rhs=ident_bf16[:], start=True, stop=True)
+            nc.scalar.activation(out=bias[:], in_=small_t[:, 0 : 2 * H], func=ACT.Identity)
 
         factor = keep.tile([P, CHUNKS, P, R], F32)
 
-        def mask_factor(c):
+        def mask_factor(c, on_vector=False):
             mask_all = psum.tile([P, R, P], F32, tag="bank")
             for r in range(R):
                 row = MASK_ROW + r * CHUNKS + c
@@ -112,50 +114,58 @@ def tile_rowselfattention_pa_kernel(tc, x, mask, Wq, bq, Wk, bk, out):
                     start=True,
                     stop=True,
                 )
-            nc.scalar.activation(
-                out=factor[:, c, :, :],
-                in_=mask_all[:].rearrange("p r i -> p i r"),
-                func=ACT.Copy,
-                bias=SCALING,
-                scale=-SCALING,
-            )
+            if on_vector:
+                nc.vector.tensor_scalar(
+                    out=factor[:, c, :, :],
+                    in0=mask_all[:].rearrange("p r i -> p i r"),
+                    scalar1=-SCALING,
+                    scalar2=SCALING,
+                    op0=ALU.mult,
+                    op1=ALU.add,
+                )
+            else:
+                nc.scalar.activation(
+                    out=factor[:, c, :, :],
+                    in_=mask_all[:].rearrange("p r i -> p i r"),
+                    func=ACT.Copy,
+                    bias=SCALING,
+                    scale=-SCALING,
+                )
 
         w_grouped = keep.tile([P, H, 2, D, PACK], BF16, align_bytes=64)
         w_codes = keep.tile([P, H, 2, D], U32, align_bytes=64)
         w_scales = keep.tile([P, H, 2, D], U8, align_bytes=64)
 
-        def regroup_w(h):
-            for which in (K, Q):
-                nc.vector.tensor_copy(
-                    out=w_grouped[:, h, which, :, :].rearrange("p (g i) t -> p g t i", i=RUN),
-                    in_=w_raw[:, which, :, h * D : (h + 1) * D].rearrange("p t (g i) -> p g t i", i=RUN),
-                )
+        def regroup_w(which, h):
+            nc.vector.tensor_copy(
+                out=w_grouped[:, h, which, :, :].rearrange("p (g i) t -> p g t i", i=RUN),
+                in_=w_raw[:, which, :, h * D : (h + 1) * D].rearrange("p t (g i) -> p g t i", i=RUN),
+            )
 
-        def quantise_w(h):
+        def quantise_w(which, h):
             nc.vector.quantize_mx(
-                out=w_codes[:, h, :, :].rearrange("p n d -> p (n d)").bitcast(FP8X4),
-                scales=w_scales[:, h, :, :].rearrange("p n d -> p (n d)"),
-                in_=w_grouped[:, h, :, :, :].rearrange("p n d t -> p (n d t)"),
+                out=w_codes[:, h, which, :].bitcast(FP8X4),
+                scales=w_scales[:, h, which, :],
+                in_=w_grouped[:, h, which, :, :].rearrange("p d t -> p (d t)"),
             )
 
         x_grouped = keep.tile([P, CHUNKS, TOKENS * PACK], BF16, align_bytes=64)
         x_codes = keep.tile([P, CHUNKS, TOKENS], U32, align_bytes=64)
         x_scales = keep.tile([P, CHUNKS, TOKENS], U8, align_bytes=64)
 
-        def transpose_x(c):
+        def transpose_x(c, pair):
             x_words = x_sb[:, c, :].bitcast(F32).rearrange("i (r u p) -> i r u p", r=R, u=2)
             grouped_words = x_grouped[:, c, :].bitcast(F32).rearrange("p (n u) -> p n u", u=2)
-            for pair in range(R // 2):
-                x_t = psum.tile([P, 2, 2 * P], F32, tag="bank")
-                for half in range(2):
-                    r = 2 * pair + half
-                    for u in range(2):
-                        nc.tensor.transpose(
-                            x_t[:, u, half * P : (half + 1) * P], x_words[:, r, u, :], ident_f32[:]
-                        )
-                tokens = slice(pair * 2 * P, (pair + 1) * 2 * P)
-                empty = nc.vector.tensor_copy if (c, pair) == (1, 1) else nc.scalar.copy
-                empty(out=grouped_words[:, tokens, :], in_=x_t[:].rearrange("p u n -> p n u"))
+            x_t = psum.tile([P, 2, 2 * P], F32, tag="bank")
+            for half in range(2):
+                r = 2 * pair + half
+                for u in range(2):
+                    nc.tensor.transpose(
+                        x_t[:, u, half * P : (half + 1) * P], x_words[:, r, u, :], ident_f32[:]
+                    )
+            tokens = slice(pair * 2 * P, (pair + 1) * 2 * P)
+            empty = nc.vector.tensor_copy if (c, pair) == (1, 1) else nc.scalar.copy
+            empty(out=grouped_words[:, tokens, :], in_=x_t[:].rearrange("p u n -> p n u"))
 
         def quantise_x(c, pair):
             tokens = slice(pair * 2 * P, (pair + 1) * 2 * P)
@@ -239,48 +249,53 @@ def tile_rowselfattention_pa_kernel(tc, x, mask, Wq, bq, Wk, bk, out):
                 nc.scalar.copy(out=result[:], in_=accs["logits", unit][:])
             nc.sync.dma_start(out=out[h, c * P : (c + 1) * P, :], in_=result[:])
 
+        keep_warm(4)
+        transpose_x(0, 0)
+        biases()
         mask_factor(0)
         mask_factor(1)
-        transpose_x(0)
-        keep_warm(2)
-        regroup_w(0)
+        transpose_x(0, 1)
+        regroup_w(K, 0)
         quantise_x(0, 0)
-        quantise_w(0)
-        mask_factor(2)
-        mask_factor(3)
+        quantise_w(K, 0)
+        regroup_w(K, 2)
+        regroup_w(K, 3)
         quantise_x(0, 1)
+        mask_factor(2)
+        mask_factor(3, on_vector=True)
 
-        regroup_at = {1: 1, 2: 2, 6: 3}
-        k_next = 0
-        k_left = []
-        for step in range(LOGITS_FIRST + LOGITS_STEPS):
+        w_quantise_at = {0: ((K, 2), (K, 3)), 1: ((Q, 0), (K, 1)), 3: ((Q, 1), (Q, 2)), 4: ((Q, 3),)}
+        w_regroup_at = {0: ((Q, 0), (K, 1)), 2: ((Q, 1), (Q, 2)), 3: ((Q, 3),)}
+        k_emptied = []
+        for step in range(Q_STEP + UNITS + LOGITS_LAG):
             if step + 1 < CHUNKS:
-                transpose_x(step + 1)
+                transpose_x(step + 1, 0)
+                transpose_x(step + 1, 1)
+                keep_warm(1)
                 quantise_x(step + 1, 0)
                 quantise_x(step + 1, 1)
-            k_last = step if step < CHUNKS else min(2 * step - CHUNKS + 1, step + AHEAD)
-            k_units = list(range(k_next, min(k_last + 1, UNITS)))
-            k_next += len(k_units)
-            for unit in k_units:
-                project(K, unit)
-            if step < UNITS:
-                project(Q, step)
-            l_units = [i for i in range(UNITS) if LOGITS_FIRST + i * LOGITS_STEPS // UNITS == step]
-            for unit in l_units:
-                multiply(unit)
-            for unit in k_left:
+            for unit in k_emptied:
                 if unit % 2 == 1:
                     quantise(K, unit - 1, 2)
-            k_left = k_units
+            k_units = [i for i in range(UNITS) if step == (i if i < CHUNKS else i - K_EARLY)]
+            q_unit = step - Q_STEP
+            l_unit = q_unit - LOGITS_LAG
+            for unit in k_units:
+                project(K, unit)
+            if 0 <= q_unit < UNITS:
+                project(Q, q_unit)
+            if l_unit >= 0:
+                multiply(l_unit)
             for unit in k_units:
                 empty_k(unit)
-            if step - 1 in regroup_at:
-                quantise_w(regroup_at[step - 1])
-            if step < UNITS:
-                empty_q(step)
-            if 1 <= step <= UNITS:
-                quantise(Q, step - 1, 1)
-            if step in regroup_at:
-                regroup_w(regroup_at[step])
-            for unit in l_units:
-                store(unit)
+            k_emptied = k_units
+            for which, h in w_quantise_at.get(step, ()):
+                quantise_w(which, h)
+            if 0 <= q_unit < UNITS:
+                empty_q(q_unit)
+            if 1 <= q_unit <= UNITS:
+                quantise(Q, q_unit - 1, 1)
+            for which, h in w_regroup_at.get(step, ()):
+                regroup_w(which, h)
+            if l_unit >= 0:
+                store(l_unit)

@@ -228,26 +228,29 @@ def tile_rowselfattention_pa_kernel(tc, x, mask, Wq, bq, Wk, bk, out):
         def multiply(unit):
             h, c = divmod(unit, CHUNKS)
             cols = slice(c * P, (c + 1) * P)
-            acc_out = psum.tile([P, C], F32, tag="bank")
-            nc.tensor.matmul_mx(
-                out=acc_out[:],
-                lhsT=codes[:, Q, h, cols].bitcast(FP8X4),
-                lhsT_scale=scales[:, Q, h, cols],
-                rhs=codes[:, K, h, :].bitcast(FP8X4),
-                rhs_scale=scales[:, K, h, :],
-                start=True,
-                stop=True,
-            )
-            accs["logits", unit] = acc_out
+            parts = 2 if unit == UNITS - 1 else 1
+            for part in range(parts):
+                keys = slice(part * C // parts, (part + 1) * C // parts)
+                acc_out = psum.tile([P, C // parts], F32, tag="bank")
+                nc.tensor.matmul_mx(
+                    out=acc_out[:],
+                    lhsT=codes[:, Q, h, cols].bitcast(FP8X4),
+                    lhsT_scale=scales[:, Q, h, cols],
+                    rhs=codes[:, K, h, keys].bitcast(FP8X4),
+                    rhs_scale=scales[:, K, h, keys],
+                    start=True,
+                    stop=True,
+                )
+                accs["logits", unit, part] = (acc_out, keys)
 
         def store(unit):
             h, c = divmod(unit, CHUNKS)
-            result = stores.tile([P, C], F32)
-            if unit == UNITS - 1:
-                nc.vector.tensor_copy(out=result[:], in_=accs["logits", unit][:])
-            else:
-                nc.scalar.copy(out=result[:], in_=accs["logits", unit][:])
-            nc.sync.dma_start(out=out[h, c * P : (c + 1) * P, :], in_=result[:])
+            for part in range(2 if unit == UNITS - 1 else 1):
+                acc_out, keys = accs["logits", unit, part]
+                result = stores.tile([P, keys.stop - keys.start], F32)
+                empty = nc.vector.tensor_copy if part == 1 else nc.scalar.copy
+                empty(out=result[:], in_=acc_out[:])
+                nc.sync.dma_start(out=out[h, c * P : (c + 1) * P, keys], in_=result[:])
 
         keep_warm(4)
         transpose_x(0, 0)

import math
from contextlib import ExitStack

import concourse.mybir as mybir
from concourse.masks import make_identity

F32 = mybir.dt.float32
BF16 = mybir.dt.bfloat16
U32 = mybir.dt.uint32
U8 = mybir.dt.uint8
FP8X4 = mybir.dt.float8_e4m3fn_x4
ACT = mybir.ActivationFunctionType
ALU = mybir.AluOpType

P = 128
PACK = 4
R, C, E, H = 4, 512, 512, 4
D = E // H
CHUNKS = C // P
TOKENS = R * P
UNITS = H * CHUNKS
BANKS = 8
RUN = 4
Q_STEP = CHUNKS
K_EARLY = 2
LOGITS_LAG = 4
SCALING = (D ** -0.5) / math.sqrt(R)
FLOPS = 2 * R * C * E * 2 * E + 2 * H * C * C * R * D

BQ_ROW = 0
BK_ROW = H
MASK_ROW = 2 * H
K, Q = 0, 1


def tile_rowselfattention_pa_kernel(tc, x, mask, Wq, bq, Wk, bk, out):
    nc = tc.nc
    with ExitStack() as ctx:
        ctx.enter_context(tc.manual_schedule())
        keep = ctx.enter_context(tc.tile_pool(name="keep", bufs=1))
        stores = ctx.enter_context(tc.tile_pool(name="stores", bufs=8))
        psum = ctx.enter_context(tc.psum_pool(name="psum", bufs=BANKS))

        zeros = keep.tile([P, C], BF16)
        nc.vector.memset(zeros[:], 0.0)
        small = keep.tile([P, P], BF16)
        nc.gpsimd.memset(small[:], 0.0)
        ident_f32 = keep.tile([P, P], F32)
        make_identity(nc, ident_f32[:])
        ident_bf16 = keep.tile([P, P], BF16)
        make_identity(nc, ident_bf16[:])

        x_sb = keep.tile([P, CHUNKS, R * E], BF16)
        w_raw = keep.tile([P, 2, PACK, E], BF16)

        def load_x(c, pair):
            rows = slice(2 * pair, 2 * pair + 2)
            nc.sync.dma_start(
                out=x_sb[:, c, :].rearrange("p (r e) -> p r e", r=R)[:, rows, :],
                in_=x[rows, c * P : (c + 1) * P, :].rearrange("r p e -> p r e"),
            )

        def load_small():
            nc.sync.dma_start(out=small[BQ_ROW : BQ_ROW + H, :], in_=bq.rearrange("(h d) -> h d", d=D))
            nc.sync.dma_start(out=small[BK_ROW : BK_ROW + H, :], in_=bk.rearrange("(h d) -> h d", d=D))
            nc.sync.dma_start(
                out=small[MASK_ROW : MASK_ROW + R * CHUNKS, :],
                in_=mask.rearrange("r (c i) -> (r c) i", i=P),
            )

        def load_w(which, first, last):
            cols = slice(first * D, last * D)
            w = Wk if which == K else Wq
            for u in range(2):
                nc.sync.dma_start(
                    out=w_raw[:, which, 2 * u : 2 * u + 2, cols],
                    in_=w[2 * u * P : 2 * (u + 1) * P, cols].rearrange("(p e) d -> p e d", e=2),
                )

        load_x(0, 0)
        load_small()
        load_x(0, 1)
        load_w(K, 0, H)
        for c in (1, 2):
            load_x(c, 0)
            load_x(c, 1)
        load_w(Q, 0, 1)
        load_x(3, 0)
        load_x(3, 1)
        load_w(Q, 1, H)

        def keep_warm(count):
            unread = psum.tile([P, C], F32, tag="bank")
            for n in range(count):
                nc.tensor.matmul(out=unread[:], lhsT=zeros[:, 0:P], rhs=zeros[:], start=True, stop=True)

        bias = keep.tile([P, 2 * H], F32)

        def biases():
            small_t = psum.tile([P, P], F32, tag="bank")
            nc.tensor.matmul(out=small_t[:], lhsT=small[:], rhs=ident_bf16[:], start=True, stop=True)
            nc.scalar.activation(out=bias[:], in_=small_t[:, 0 : 2 * H], func=ACT.Identity)

        factor = keep.tile([P, CHUNKS, P, R], F32)

        def mask_factor(c, on_vector=False):
            mask_all = psum.tile([P, R, P], F32, tag="bank")
            for r in range(R):
                row = MASK_ROW + r * CHUNKS + c
                nc.tensor.matmul(
                    out=mask_all[:, r, :],
                    lhsT=ident_bf16[:, row : row + 1].to_broadcast([P, P]),
                    rhs=small[:],
                    start=True,
                    stop=True,
                )
            if on_vector:
                nc.vector.tensor_scalar(
                    out=factor[:, c, :, :],
                    in0=mask_all[:].rearrange("p r i -> p i r"),
                    scalar1=-SCALING,
                    scalar2=SCALING,
                    op0=ALU.mult,
                    op1=ALU.add,
                )
            else:
                nc.scalar.activation(
                    out=factor[:, c, :, :],
                    in_=mask_all[:].rearrange("p r i -> p i r"),
                    func=ACT.Copy,
                    bias=SCALING,
                    scale=-SCALING,
                )

        w_grouped = keep.tile([P, H, 2, D, PACK], BF16, align_bytes=64)
        w_codes = keep.tile([P, H, 2, D], U32, align_bytes=64)
        w_scales = keep.tile([P, H, 2, D], U8, align_bytes=64)

        def regroup_w(which, h):
            nc.vector.tensor_copy(
                out=w_grouped[:, h, which, :, :].rearrange("p (g i) t -> p g t i", i=RUN),
                in_=w_raw[:, which, :, h * D : (h + 1) * D].rearrange("p t (g i) -> p g t i", i=RUN),
            )

        def quantise_w(which, h):
            nc.vector.quantize_mx(
                out=w_codes[:, h, which, :].bitcast(FP8X4),
                scales=w_scales[:, h, which, :],
                in_=w_grouped[:, h, which, :, :].rearrange("p d t -> p (d t)"),
            )

        x_grouped = keep.tile([P, CHUNKS, TOKENS * PACK], BF16, align_bytes=64)
        x_codes = keep.tile([P, CHUNKS, TOKENS], U32, align_bytes=64)
        x_scales = keep.tile([P, CHUNKS, TOKENS], U8, align_bytes=64)

        def transpose_x(c, pair):
            x_words = x_sb[:, c, :].bitcast(F32).rearrange("i (r u p) -> i r u p", r=R, u=2)
            grouped_words = x_grouped[:, c, :].bitcast(F32).rearrange("p (n u) -> p n u", u=2)
            x_t = psum.tile([P, 2, 2 * P], F32, tag="bank")
            for half in range(2):
                r = 2 * pair + half
                for u in range(2):
                    nc.tensor.transpose(
                        x_t[:, u, half * P : (half + 1) * P], x_words[:, r, u, :], ident_f32[:]
                    )
            tokens = slice(pair * 2 * P, (pair + 1) * 2 * P)
            empty = nc.vector.tensor_copy if (c, pair) == (1, 1) else nc.scalar.copy
            empty(out=grouped_words[:, tokens, :], in_=x_t[:].rearrange("p u n -> p n u"))

        def quantise_x(c, pair):
            tokens = slice(pair * 2 * P, (pair + 1) * 2 * P)
            nc.vector.quantize_mx(
                out=x_codes[:, c, tokens].bitcast(FP8X4),
                scales=x_scales[:, c, tokens],
                in_=x_grouped[:, c, pair * 2 * P * PACK : (pair + 1) * 2 * P * PACK],
            )

        grouped = keep.tile([P, 2, H, CHUNKS, P * R], BF16, align_bytes=64)
        codes = keep.tile([P, 2, H, C], U32, align_bytes=64)
        scales = keep.tile([P, 2, H, C], U8, align_bytes=64)

        accs = {}

        def project(which, unit):
            h, c = divmod(unit, CHUNKS)
            acc = psum.tile([P, R, P], F32, tag="bank")
            nc.tensor.matmul_mx(
                out=acc[:].rearrange("p r i -> p (r i)"),
                lhsT=w_codes[:, h, which, :].bitcast(FP8X4),
                lhsT_scale=w_scales[:, h, which, :],
                rhs=x_codes[:, c, :].bitcast(FP8X4),
                rhs_scale=x_scales[:, c, :],
                start=True,
                stop=True,
            )
            accs[which, unit] = acc

        def empty_k(unit):
            h, c = divmod(unit, CHUNKS)
            nc.scalar.activation(
                out=grouped[:, K, h, c, :].rearrange("p (i r) -> p i r", r=R),
                in_=accs[K, unit][:].rearrange("p r i -> p i r"),
                func=ACT.Identity,
                bias=bias[:, BK_ROW + h : BK_ROW + h + 1],
                scale=1.0,
            )

        def empty_q(unit):
            h, c = divmod(unit, CHUNKS)
            nc.vector.scalar_tensor_tensor(
                out=grouped[:, Q, h, c, :].rearrange("p (i r) -> p i r", r=R),
                in0=accs[Q, unit][:].rearrange("p r i -> p i r"),
                scalar=bias[:, BQ_ROW + h : BQ_ROW + h + 1],
                in1=factor[:, c, :, :],
                op0=ALU.add,
                op1=ALU.mult,
            )

        def quantise(which, first, count):
            h, c = divmod(first, CHUNKS)
            cols = slice(c * P, (c + count) * P)
            nc.vector.quantize_mx(
                out=codes[:, which, h, cols].bitcast(FP8X4),
                scales=scales[:, which, h, cols],
                in_=grouped[:, which, h, c : c + count, :].rearrange("p c n -> p (c n)"),
            )

        def multiply(unit):
            h, c = divmod(unit, CHUNKS)
            cols = slice(c * P, (c + 1) * P)
            parts = 2 if unit == UNITS - 1 else 1
            for part in range(parts):
                keys = slice(part * C // parts, (part + 1) * C // parts)
                acc_out = psum.tile([P, C // parts], F32, tag="bank")
                nc.tensor.matmul_mx(
                    out=acc_out[:],
                    lhsT=codes[:, Q, h, cols].bitcast(FP8X4),
                    lhsT_scale=scales[:, Q, h, cols],
                    rhs=codes[:, K, h, keys].bitcast(FP8X4),
                    rhs_scale=scales[:, K, h, keys],
                    start=True,
                    stop=True,
                )
                accs["logits", unit, part] = (acc_out, keys)

        def store(unit):
            h, c = divmod(unit, CHUNKS)
            for part in range(2 if unit == UNITS - 1 else 1):
                acc_out, keys = accs["logits", unit, part]
                result = stores.tile([P, keys.stop - keys.start], F32)
                empty = nc.vector.tensor_copy if part == 1 else nc.scalar.copy
                empty(out=result[:], in_=acc_out[:])
                nc.sync.dma_start(out=out[h, c * P : (c + 1) * P, keys], in_=result[:])

        keep_warm(4)
        transpose_x(0, 0)
        biases()
        mask_factor(0)
        mask_factor(1)
        transpose_x(0, 1)
        regroup_w(K, 0)
        quantise_x(0, 0)
        quantise_w(K, 0)
        regroup_w(K, 2)
        regroup_w(K, 3)
        quantise_x(0, 1)
        mask_factor(2)
        mask_factor(3, on_vector=True)

        w_quantise_at = {0: ((K, 2), (K, 3)), 1: ((Q, 0), (K, 1)), 3: ((Q, 1), (Q, 2)), 4: ((Q, 3),)}
        w_regroup_at = {0: ((Q, 0), (K, 1)), 2: ((Q, 1), (Q, 2)), 3: ((Q, 3),)}
        k_emptied = []
        for step in range(Q_STEP + UNITS + LOGITS_LAG):
            if step + 1 < CHUNKS:
                transpose_x(step + 1, 0)
                transpose_x(step + 1, 1)
                keep_warm(1)
                quantise_x(step + 1, 0)
                quantise_x(step + 1, 1)
            for unit in k_emptied:
                if unit % 2 == 1:
                    quantise(K, unit - 1, 2)
            k_units = [i for i in range(UNITS) if step == (i if i < CHUNKS else i - K_EARLY)]
            q_unit = step - Q_STEP
            l_unit = q_unit - LOGITS_LAG
            for unit in k_units:
                project(K, unit)
            if 0 <= q_unit < UNITS:
                project(Q, q_unit)
            if l_unit >= 0:
                multiply(l_unit)
            for unit in k_units:
                empty_k(unit)
            k_emptied = k_units
            for which, h in w_quantise_at.get(step, ()):
                quantise_w(which, h)
            if 0 <= q_unit < UNITS:
                empty_q(q_unit)
            if 1 <= q_unit <= UNITS:
                quantise(Q, q_unit - 1, 1)
            for which, h in w_regroup_at.get(step, ()):
                regroup_w(which, h)
            if l_unit >= 0:
                store(l_unit)
